import numpy as np
import ml_dtypes


def mxq(x, axis, fmt="e4m3"):
    dtype, down = {"e4m3": (ml_dtypes.float8_e4m3fn, 7), "e5m2": (ml_dtypes.float8_e5m2, 14)}[fmt]
    v = np.moveaxis(np.asarray(x, np.float32).astype(ml_dtypes.bfloat16).astype(np.float64), axis, -1)
    blocks = v.reshape(v.shape[:-1] + (-1, 32))
    amax = np.abs(blocks).max(-1, keepdims=True)
    byte = np.maximum(np.where(amax > 0, np.frexp(amax)[1] - 1 + 127, 0) - down, 1)
    scale = np.exp2(byte - 127.0)
    codes = (blocks / scale).astype(np.float32).astype(dtype).astype(np.float64)
    return np.moveaxis((codes * scale).reshape(v.shape), -1, axis)


WIDE = False


def mx_kscale(k):
    if not WIDE:
        return np.ones(k)
    levels = np.array([10, -10, 5, -5, 0])
    a = np.random.permutation(np.resize(levels, k // 512 * 4)).reshape(k // 512, 4)
    idx = np.arange(k)
    return np.exp2(a[idx // 512, idx % 128 // 32])


BF16 = ml_dtypes.bfloat16


def bf(x):
    return np.asarray(x, np.float32).astype(BF16)


def f64(x):
    return np.asarray(x).astype(np.float64)


B, S, DI, DO = 4, 256, 2048, 2048
R = B * S
LN_EPS = 1e-5


def ste_sign(w):
    return np.where(w >= 0, 1.0, -1.0)


def setup_inputs():
    r = np.asarray(mx_kscale(DI), np.float64)[np.arange(R) * DI // R]
    return {"x": bf(np.random.standard_normal((B, S, DI)) * r.reshape(B, S, 1)),
            "weight": bf(np.random.standard_normal((DO, DI)) * 0.02),
            "in_channel_scale": bf(np.random.uniform(0.5, 1.5, DI) / np.sqrt(DI)),
            "out_channel_scale": bf(np.random.uniform(0.5, 1.5, DO) / r.min()),
            "bias": bf(np.random.standard_normal(DO) * 0.3),
            "ln_gamma": bf(1.0 + 0.1 * np.random.standard_normal(DO)),
            "ln_beta": bf(0.1 * np.random.standard_normal(DO))}


def reference(x, weight, in_channel_scale, out_channel_scale, bias, ln_gamma, ln_beta):
    x = f64(x)
    orig_shape = x.shape
    xf = x.reshape(-1, orig_shape[-1])
    w_bin = ste_sign(f64(weight))
    xs = xf * f64(in_channel_scale)
    h = (mxq(xs, 1, "e4m3") @ mxq(w_bin, 1, "e4m3").T) * f64(out_channel_scale)
    h = h + f64(bias)
    mu = np.mean(h, axis=-1, keepdims=True)
    var = np.mean(np.square(h - mu), axis=-1, keepdims=True)
    h = (h - mu) / np.sqrt(var + LN_EPS) * f64(ln_gamma) + f64(ln_beta)
    return h.reshape(*orig_shape[:-1], weight.shape[0])

@@ -1,0 +1,197 @@
+from contextlib import ExitStack
+
+import concourse.mybir as mybir
+from concourse.masks import make_identity
+
+F32 = mybir.dt.float32
+BF16 = mybir.dt.bfloat16
+U32 = mybir.dt.uint32
+U8 = mybir.dt.uint8
+FP8X4 = mybir.dt.float8_e4m3fn_x4
+ALU = mybir.AluOpType
+ACT = mybir.ActivationFunctionType
+
+P = 128
+R, DI, DO = 1024, 2048, 2048
+FLOPS = 2 * R * DI * DO
+LN_EPS = 1e-5
+BIG = 2.0 ** 100
+TINY = 2.0 ** -40
+W_ON_S = (2, 5, 8, 10, 12, 14)
+V4_ON_V = (7,)
+
+
+def tile_onebitlinear_kernel(tc, x, weight, in_channel_scale, out_channel_scale, bias, ln_gamma, ln_beta, out):
+    nc = tc.nc
+    xf = x.flatten_outer_dims()
+    of = out.flatten_outer_dims()
+    with ExitStack() as es:
+        const = es.enter_context(tc.tile_pool(name="const", bufs=1))
+        keep = es.enter_context(tc.tile_pool(name="keep", bufs=1))
+        xin = es.enter_context(tc.tile_pool(name="xin", bufs=4))
+        xgp = es.enter_context(tc.tile_pool(name="xgp", bufs=1))
+        win = es.enter_context(tc.tile_pool(name="win", bufs=4))
+        wgp = es.enter_context(tc.tile_pool(name="wgp", bufs=3))
+        res = es.enter_context(tc.tile_pool(name="res", bufs=3))
+        small = es.enter_context(tc.tile_pool(name="small", bufs=4))
+        psa = es.enter_context(tc.psum_pool(name="psa", bufs=6))
+        psm = es.enter_context(tc.psum_pool(name="psm", bufs=2))
+
+        tiny = const.tile([P, 1], F32, name="tiny")
+        nc.vector.memset(tiny[:], TINY)
+        eps = const.tile([P, 1], F32, name="eps")
+        nc.vector.memset(eps[:], LN_EPS)
+        warm = const.tile([P, 1], F32, name="warm")
+        nc.scalar.activation(out=warm[:], in_=tiny[:], func=ACT.Sign)
+        ident_f = const.tile([P, P], F32, name="ident_f")
+        make_identity(nc, ident_f[:])
+        ident_b = const.tile([P, P], BF16, name="ident_b")
+        make_identity(nc, ident_b[:])
+        cz = const.tile([P, P], F32, name="cz")
+        nc.vector.memset(cz[:], 0.0)
+        nc.scalar.dma_start(out=cz[0:8, :].bitcast(BF16), in_=in_channel_scale.rearrange("(a b) -> a b", a=8))
+        cb = const.tile([P, P], BF16, name="cb")
+        nc.vector.memset(cb[:], 0.0)
+        nc.scalar.dma_start(out=cb[0:16, :], in_=out_channel_scale.rearrange("(a b) -> a b", a=16))
+        nc.scalar.dma_start(out=cb[16:32, :], in_=bias.rearrange("(a b) -> a b", a=16))
+        pz = psa.tile([P, 512], F32, tag="a", name="pz")
+        nc.tensor.transpose(pz[:, 0:P], cz[:], ident_f[:])
+        isc_w = const.tile([P, 8], F32, name="isc_w")
+        nc.vector.tensor_copy(out=isc_w[:], in_=pz[:, 0:8])
+        isc = isc_w[:].bitcast(BF16)
+        pb = psa.tile([P, 1024], BF16, tag="a", name="pb")
+        nc.tensor.transpose(pb[:, 0:P], cb[:], ident_b[:])
+        ob = const.tile([P, 32], F32, name="ob")
+        nc.vector.tensor_copy(out=ob[:], in_=pb[:, 0:32])
+
+        xc = keep.tile([P, 2, 4, 512], U32, align_bytes=64, name="xc")
+        xsc = keep.tile([P, 2, 4, 512], U8, align_bytes=64, name="xsc")
+        wc = keep.tile([P, 16, 4, P], U32, align_bytes=64, name="wc")
+        wsc = keep.tile([P, 16, 4, P], U8, align_bytes=64, name="wsc")
+        hT = keep.tile([P, 16, R], F32, name="hT")
+
+        def transposes(src_words, hb, nm):
+            tp = psa.tile([P, 512], F32, tag="a", name=nm)
+            for s in range(4):
+                a = 4 * hb + s
+                nc.tensor.transpose(tp[:, s * P:(s + 1) * P], src_words[:, a * P:(a + 1) * P], ident_f[:])
+            return tp
+
+        def x_block(rb, xg):
+            rl = rb % 4
+            xb = xin.tile([P, DI], BF16, name="xb")
+            nc.sync.dma_start(out=xb[:], in_=xf[rb * P:(rb + 1) * P, :])
+            xw = xb[:].bitcast(F32)
+            for hb in range(2):
+                tp = transposes(xw, hb, "tpx")
+                for gl in range(2):
+                    g = 2 * hb + gl
+                    nc.vector.tensor_tensor(
+                        out=xg[:, g, rl * P:(rl + 1) * P, :].rearrange("p r (u e) -> p r u e", u=2),
+                        in0=tp[:, gl * 256:(gl + 1) * 256].bitcast(BF16).rearrange("p (u r e) -> p r u e", u=2, e=2),
+                        in1=isc[:, 4 * g:4 * g + 4].rearrange("p (u e) -> p u e", u=2).unsqueeze(1).to_broadcast([P, P, 2, 2]),
+                        op=ALU.mult,
+                    )
+
+        def x_quant(h, xg):
+            for j in range(2):
+                nc.vector.quantize_mx(
+                    out=xc[:, h, 2 * j:2 * j + 2, :].rearrange("p g r -> p (g r)").bitcast(FP8X4),
+                    scales=xsc[:, h, 2 * j:2 * j + 2, :].rearrange("p g r -> p (g r)"),
+                    in_=xg[:, 2 * j:2 * j + 2, :, :].rearrange("p g r t -> p (g r t)"),
+                )
+
+        def w_prep(oc):
+            wt = win.tile([P, DI], BF16, tag="wt", name="wt")
+            nc.sync.dma_start(out=wt[:], in_=weight[oc * P:(oc + 1) * P, :])
+            on_s = oc in W_ON_S
+            if not on_s:
+                nc.vector.tensor_scalar(out=wt[:], in0=wt[:], scalar1=0.0, scalar2=2.0, op0=ALU.is_ge, op1=ALU.mult)
+                nc.vector.tensor_scalar_add(out=wt[:], in0=wt[:], scalar1=-1.0)
+            ww = wt[:].bitcast(F32)
+            wg = wgp.tile([P, DI], BF16, align_bytes=64, name="wg")
+            for hb in range(2):
+                tp = transposes(ww, hb, "tpw")
+                if on_s:
+                    for gl in range(2):
+                        g = 2 * hb + gl
+                        nc.scalar.activation(
+                            out=wg[:, g * 512:(g + 1) * 512].rearrange("p (o u e) -> p o u e", u=2, e=2),
+                            in_=tp[:, gl * 256:(gl + 1) * 256].bitcast(BF16).rearrange("p (u o e) -> p o u e", u=2, e=2),
+                            func=ACT.Sign, scale=BIG, bias=tiny[:],
+                        )
+                else:
+                    nc.scalar.copy(
+                        out=wg[:].bitcast(F32)[:, hb * 512:(hb + 1) * 512].rearrange("p (g o u) -> p g o u", g=2, u=2),
+                        in_=tp[:].rearrange("p (g u o) -> p g o u", g=2, u=2),
+                    )
+            nc.vector.quantize_mx(
+                out=wc[:, oc, :, :].rearrange("p g o -> p (g o)").bitcast(FP8X4),
+                scales=wsc[:, oc, :, :].rearrange("p g o -> p (g o)"),
+                in_=wg[:],
+            )
+
+        def mx_t1(oc, h):
+            acc = psm.tile([P, 512], F32, name="acc")
+            for g in range(4):
+                nc.tensor.matmul_mx(
+                    out=acc[:],
+                    lhsT=wc[:, oc, g, :].bitcast(FP8X4), lhsT_scale=wsc[:, oc, g, :],
+                    rhs=xc[:, h, g, :].bitcast(FP8X4), rhs_scale=xsc[:, h, g, :],
+                    start=(g == 0), stop=(g == 3),
+                )
+            nc.scalar.activation(out=hT[:, oc, h * 512:(h + 1) * 512], in_=acc[:], func=ACT.Identity,
+                                 scale=ob[:, oc:oc + 1], bias=ob[:, 16 + oc:17 + oc])
+
+        def ln_block(rb, g_bc, beta_bc):
+            hn = []
+            for j in range(4):
+                bank = psa.tile([P, 512], F32, tag="a", name="hn%d" % j)
+                for q in range(4):
+                    nc.tensor.transpose(bank[:, q * P:(q + 1) * P], hT[:, 4 * j + q, rb * P:(rb + 1) * P], ident_f[:])
+                hn.append(bank)
+            st = small.tile([P, 4, 6], F32, name="st")
+            for j in range(4):
+                nc.vector.bn_stats(out=st[:, j, :], in_=hn[j][:])
+            mv = small.tile([P, 2], F32, name="mv")
+            nc.vector.bn_aggr(out=mv[:], in_=st[:].rearrange("p a b -> p (a b)"))
+            sd = small.tile([P, 1], F32, name="sd")
+            nc.scalar.activation(out=sd[:], in_=mv[:, 1:2], func=ACT.Sqrt, bias=eps[:], scale=1.0)
+            rstd = small.tile([P, 1], F32, name="rstd")
+            nc.vector.reciprocal(out=rstd[:], in_=sd[:])
+            t = res.tile([P, DO], F32, name="t")
+            for j in range(4):
+                nc.vector.scalar_tensor_tensor(out=t[:, j * 512:(j + 1) * 512], in0=hn[j][:], scalar=mv[:, 0:1],
+                                               in1=g_bc[:, j * 512:(j + 1) * 512], op0=ALU.subtract, op1=ALU.mult)
+            if rb in V4_ON_V:
+                nc.vector.scalar_tensor_tensor(out=t[:], in0=t[:], scalar=rstd[:], in1=beta_bc[:], op0=ALU.mult, op1=ALU.add)
+            else:
+                nc.scalar.activation(out=t[:], in_=t[:], func=ACT.Copy, scale=rstd[:])
+                nc.gpsimd.tensor_tensor(out=t[:], in0=t[:], in1=beta_bc[:], op=ALU.add)
+            nc.sync.dma_start(out=of[rb * P:(rb + 1) * P, :], in_=t[:])
+
+        xg0 = xgp.tile([P, 4, 512, 4], BF16, align_bytes=64, name="xg")
+        for rb in range(4):
+            x_block(rb, xg0)
+        x_quant(0, xg0)
+        w_prep(0)
+        w_prep(1)
+        xg1 = xgp.tile([P, 4, 512, 4], BF16, align_bytes=64, name="xg")
+        for oc in range(16):
+            if oc + 2 < 16:
+                w_prep(oc + 2)
+            if oc in (1, 4, 7, 10):
+                x_block(4 + (oc - 1) // 3, xg1)
+            if oc == 12:
+                x_quant(1, xg1)
+            mx_t1(oc, 0)
+        g_bc = win.tile([P, DO], BF16, tag="wt", name="g_bc")
+        nc.sync.dma_start(out=g_bc[:], in_=ln_gamma.partition_broadcast(P))
+        beta_bc = win.tile([P, DO], BF16, tag="wt", name="beta_bc")
+        nc.sync.dma_start(out=beta_bc[:], in_=ln_beta.partition_broadcast(P))
+        for i in range(4):
+            for oc in range(4 * i, 4 * i + 4):
+                mx_t1(oc, 1)
+            ln_block(i, g_bc, beta_bc)
+        for i in range(4, 8):
+            ln_block(i, g_bc, beta_bc)

@@ -17,8 +17,12 @@ FLOPS = 2 * R * DI * DO
 LN_EPS = 1e-5
 BIG = 2.0 ** 100
 TINY = 2.0 ** -40
-W_ON_S = (2, 5, 8, 10, 12, 14)
-V4_ON_V = (7,)
+W_ON_V = (3, 6, 9, 12, 14)
+AHEAD = 3
+X_AT = {1: 3, 4: 4, 7: 5, 10: 6, 13: 7}
+EXTRA_FROM = 5
+EXTRA = 6
+UNITS = 7
 
 
 def tile_onebitlinear_kernel(tc, x, weight, in_channel_scale, out_channel_scale, bias, ln_gamma, ln_beta, out):
@@ -29,61 +33,67 @@ def tile_onebitlinear_kernel(tc, x, weight, in_channel_scale, out_channel_scale,
         const = es.enter_context(tc.tile_pool(name="const", bufs=1))
         keep = es.enter_context(tc.tile_pool(name="keep", bufs=1))
         xin = es.enter_context(tc.tile_pool(name="xin", bufs=4))
-        xgp = es.enter_context(tc.tile_pool(name="xgp", bufs=1))
-        win = es.enter_context(tc.tile_pool(name="win", bufs=4))
-        wgp = es.enter_context(tc.tile_pool(name="wgp", bufs=3))
+        xgp = es.enter_context(tc.tile_pool(name="xgp", bufs=2))
+        win = es.enter_context(tc.tile_pool(name="win", bufs=6))
+        wgp = es.enter_context(tc.tile_pool(name="wgp", bufs=4))
         res = es.enter_context(tc.tile_pool(name="res", bufs=3))
         small = es.enter_context(tc.tile_pool(name="small", bufs=4))
         psa = es.enter_context(tc.psum_pool(name="psa", bufs=6))
         psm = es.enter_context(tc.psum_pool(name="psm", bufs=2))
+        es.enter_context(tc.manual_schedule())
 
+        cz = const.tile([P, P], F32, name="cz")
+        nc.vector.memset(cz[:], 0.0)
+        nc.sync.dma_start(out=cz[0:8, :].bitcast(BF16), in_=in_channel_scale.rearrange("(a b) -> a b", a=8))
         tiny = const.tile([P, 1], F32, name="tiny")
         nc.vector.memset(tiny[:], TINY)
         eps = const.tile([P, 1], F32, name="eps")
         nc.vector.memset(eps[:], LN_EPS)
+        cb = const.tile([P, P], BF16, name="cb")
+        nc.vector.memset(cb[:], 0.0)
+        nc.scalar.dma_start(out=cb[0:16, :], in_=out_channel_scale.rearrange("(a b) -> a b", a=16))
+        nc.scalar.dma_start(out=cb[16:32, :], in_=bias.rearrange("(a b) -> a b", a=16))
         warm = const.tile([P, 1], F32, name="warm")
         nc.scalar.activation(out=warm[:], in_=tiny[:], func=ACT.Sign)
         ident_f = const.tile([P, P], F32, name="ident_f")
         make_identity(nc, ident_f[:])
         ident_b = const.tile([P, P], BF16, name="ident_b")
         make_identity(nc, ident_b[:])
-        cz = const.tile([P, P], F32, name="cz")
-        nc.vector.memset(cz[:], 0.0)
-        nc.scalar.dma_start(out=cz[0:8, :].bitcast(BF16), in_=in_channel_scale.rearrange("(a b) -> a b", a=8))
-        cb = const.tile([P, P], BF16, name="cb")
-        nc.vector.memset(cb[:], 0.0)
-        nc.scalar.dma_start(out=cb[0:16, :], in_=out_channel_scale.rearrange("(a b) -> a b", a=16))
-        nc.scalar.dma_start(out=cb[16:32, :], in_=bias.rearrange("(a b) -> a b", a=16))
-        pz = psa.tile([P, 512], F32, tag="a", name="pz")
-        nc.tensor.transpose(pz[:, 0:P], cz[:], ident_f[:])
         isc_w = const.tile([P, 8], F32, name="isc_w")
-        nc.vector.tensor_copy(out=isc_w[:], in_=pz[:, 0:8])
         isc = isc_w[:].bitcast(BF16)
-        pb = psa.tile([P, 1024], BF16, tag="a", name="pb")
-        nc.tensor.transpose(pb[:, 0:P], cb[:], ident_b[:])
         ob = const.tile([P, 32], F32, name="ob")
-        nc.vector.tensor_copy(out=ob[:], in_=pb[:, 0:32])
 
-        xc = keep.tile([P, 2, 4, 512], U32, align_bytes=64, name="xc")
-        xsc = keep.tile([P, 2, 4, 512], U8, align_bytes=64, name="xsc")
+        xc = keep.tile([P, 4, 4, 256], U32, align_bytes=64, name="xc")
+        xsc = keep.tile([P, 4, 4, 256], U8, align_bytes=64, name="xsc")
         wc = keep.tile([P, 16, 4, P], U32, align_bytes=64, name="wc")
         wsc = keep.tile([P, 16, 4, P], U8, align_bytes=64, name="wsc")
         hT = keep.tile([P, 16, R], F32, name="hT")
 
-        def transposes(src_words, hb, nm):
-            tp = psa.tile([P, 512], F32, tag="a", name=nm)
-            for s in range(4):
-                a = 4 * hb + s
-                nc.tensor.transpose(tp[:, s * P:(s + 1) * P], src_words[:, a * P:(a + 1) * P], ident_f[:])
-            return tp
+        xb, wt, tps, wg, acc, banks, stat, ln = {}, {}, {}, {}, {}, {}, {}, {}
 
-        def x_block(rb, xg):
-            rl = rb % 4
-            xb = xin.tile([P, DI], BF16, name="xb")
-            nc.sync.dma_start(out=xb[:], in_=xf[rb * P:(rb + 1) * P, :])
-            xw = xb[:].bitcast(F32)
+        def load_x(rb):
+            t = xin.tile([P, DI], BF16, name="xb")
+            nc.sync.dma_start(out=t[:], in_=xf[rb * P:(rb + 1) * P, :])
+            xb[rb] = t
+
+        def load_w(oc):
+            t = win.tile([P, DI], BF16, tag="wt", name="wt")
+            nc.sync.dma_start(out=t[:], in_=weight[oc * P:(oc + 1) * P, :])
+            wt[oc] = t
+
+        def transposes(src, key):
+            words = src[:].bitcast(F32)
             for hb in range(2):
-                tp = transposes(xw, hb, "tpx")
+                tp = psa.tile([P, 512], F32, tag="a", name="tp")
+                for s in range(4):
+                    a = 4 * hb + s
+                    nc.tensor.transpose(tp[:, s * P:(s + 1) * P], words[:, a * P:(a + 1) * P], ident_f[:])
+                tps[key, hb] = tp
+
+        def x_mult(rb, xg):
+            rl = rb % 2
+            for hb in range(2):
+                tp = tps[("x", rb), hb]
                 for gl in range(2):
                     g = 2 * hb + gl
                     nc.vector.tensor_tensor(
@@ -93,105 +103,196 @@ def tile_onebitlinear_kernel(tc, x, weight, in_channel_scale, out_channel_scale,
                         op=ALU.mult,
                     )
 
-        def x_quant(h, xg):
+        def x_quant(q, xg):
             for j in range(2):
                 nc.vector.quantize_mx(
-                    out=xc[:, h, 2 * j:2 * j + 2, :].rearrange("p g r -> p (g r)").bitcast(FP8X4),
-                    scales=xsc[:, h, 2 * j:2 * j + 2, :].rearrange("p g r -> p (g r)"),
+                    out=xc[:, q, 2 * j:2 * j + 2, :].rearrange("p g r -> p (g r)").bitcast(FP8X4),
+                    scales=xsc[:, q, 2 * j:2 * j + 2, :].rearrange("p g r -> p (g r)"),
                     in_=xg[:, 2 * j:2 * j + 2, :, :].rearrange("p g r t -> p (g r t)"),
                 )
 
-        def w_prep(oc):
-            wt = win.tile([P, DI], BF16, tag="wt", name="wt")
-            nc.sync.dma_start(out=wt[:], in_=weight[oc * P:(oc + 1) * P, :])
-            on_s = oc in W_ON_S
-            if not on_s:
-                nc.vector.tensor_scalar(out=wt[:], in0=wt[:], scalar1=0.0, scalar2=2.0, op0=ALU.is_ge, op1=ALU.mult)
-                nc.vector.tensor_scalar_add(out=wt[:], in0=wt[:], scalar1=-1.0)
-            ww = wt[:].bitcast(F32)
-            wg = wgp.tile([P, DI], BF16, align_bytes=64, name="wg")
-            for hb in range(2):
-                tp = transposes(ww, hb, "tpw")
-                if on_s:
-                    for gl in range(2):
-                        g = 2 * hb + gl
-                        nc.scalar.activation(
-                            out=wg[:, g * 512:(g + 1) * 512].rearrange("p (o u e) -> p o u e", u=2, e=2),
-                            in_=tp[:, gl * 256:(gl + 1) * 256].bitcast(BF16).rearrange("p (u o e) -> p o u e", u=2, e=2),
-                            func=ACT.Sign, scale=BIG, bias=tiny[:],
-                        )
+        def w_exit(oc):
+            wg[oc] = wgp.tile([P, DI], BF16, align_bytes=64, name="wg")
+            for g in range(4):
+                tp = tps[("w", oc), g // 2]
+                gl = g % 2
+                dst = wg[oc][:, g * 512:(g + 1) * 512].rearrange("p (o u e) -> p o u e", u=2, e=2)
+                src = tp[:, gl * 256:(gl + 1) * 256].bitcast(BF16).rearrange("p (u o e) -> p o u e", u=2, e=2)
+                if oc in W_ON_V:
+                    nc.vector.tensor_scalar(out=dst, in0=src, scalar1=0.0, scalar2=2.0, op0=ALU.is_ge, op1=ALU.mult)
                 else:
-                    nc.scalar.copy(
-                        out=wg[:].bitcast(F32)[:, hb * 512:(hb + 1) * 512].rearrange("p (g o u) -> p g o u", g=2, u=2),
-                        in_=tp[:].rearrange("p (g u o) -> p g o u", g=2, u=2),
-                    )
+                    nc.scalar.activation(out=dst, in_=src, func=ACT.Sign, scale=BIG, bias=tiny[:])
+            if oc in W_ON_V:
+                nc.vector.tensor_scalar_add(out=wg[oc][:], in0=wg[oc][:], scalar1=-1.0)
+
+        def w_quant(oc):
             nc.vector.quantize_mx(
                 out=wc[:, oc, :, :].rearrange("p g o -> p (g o)").bitcast(FP8X4),
                 scales=wsc[:, oc, :, :].rearrange("p g o -> p (g o)"),
-                in_=wg[:],
+                in_=wg[oc][:],
             )
 
-        def mx_t1(oc, h):
-            acc = psm.tile([P, 512], F32, name="acc")
+        def mx(oc, q):
+            a = psm.tile([P, 256], F32, name="acc")
             for g in range(4):
                 nc.tensor.matmul_mx(
-                    out=acc[:],
+                    out=a[:],
                     lhsT=wc[:, oc, g, :].bitcast(FP8X4), lhsT_scale=wsc[:, oc, g, :],
-                    rhs=xc[:, h, g, :].bitcast(FP8X4), rhs_scale=xsc[:, h, g, :],
+                    rhs=xc[:, q, g, :].bitcast(FP8X4), rhs_scale=xsc[:, q, g, :],
                     start=(g == 0), stop=(g == 3),
                 )
-            nc.scalar.activation(out=hT[:, oc, h * 512:(h + 1) * 512], in_=acc[:], func=ACT.Identity,
+            acc[oc, q] = a
+
+        def affine(oc, q):
+            nc.scalar.activation(out=hT[:, oc, q * 256:(q + 1) * 256], in_=acc[oc, q][:], func=ACT.Identity,
                                  scale=ob[:, oc:oc + 1], bias=ob[:, 16 + oc:17 + oc])
 
-        def ln_block(rb, g_bc, beta_bc):
-            hn = []
-            for j in range(4):
-                bank = psa.tile([P, 512], F32, tag="a", name="hn%d" % j)
-                for q in range(4):
-                    nc.tensor.transpose(bank[:, q * P:(q + 1) * P], hT[:, 4 * j + q, rb * P:(rb + 1) * P], ident_f[:])
-                hn.append(bank)
+        def ln_tr(rb, j):
+            bank = psa.tile([P, 512], F32, tag="a", name="hn")
+            for q in range(4):
+                nc.tensor.transpose(bank[:, q * P:(q + 1) * P], hT[:, 4 * j + q, rb * P:(rb + 1) * P], ident_f[:])
+            banks[rb, j] = bank
+
+        def ln_stats(rb):
             st = small.tile([P, 4, 6], F32, name="st")
             for j in range(4):
-                nc.vector.bn_stats(out=st[:, j, :], in_=hn[j][:])
+                nc.vector.bn_stats(out=st[:, j, :], in_=banks[rb, j][:])
             mv = small.tile([P, 2], F32, name="mv")
             nc.vector.bn_aggr(out=mv[:], in_=st[:].rearrange("p a b -> p (a b)"))
             sd = small.tile([P, 1], F32, name="sd")
             nc.scalar.activation(out=sd[:], in_=mv[:, 1:2], func=ACT.Sqrt, bias=eps[:], scale=1.0)
             rstd = small.tile([P, 1], F32, name="rstd")
-            nc.vector.reciprocal(out=rstd[:], in_=sd[:])
             t = res.tile([P, DO], F32, name="t")
-            for j in range(4):
-                nc.vector.scalar_tensor_tensor(out=t[:, j * 512:(j + 1) * 512], in0=hn[j][:], scalar=mv[:, 0:1],
-                                               in1=g_bc[:, j * 512:(j + 1) * 512], op0=ALU.subtract, op1=ALU.mult)
-            if rb in V4_ON_V:
-                nc.vector.scalar_tensor_tensor(out=t[:], in0=t[:], scalar=rstd[:], in1=beta_bc[:], op0=ALU.mult, op1=ALU.add)
-            else:
-                nc.scalar.activation(out=t[:], in_=t[:], func=ACT.Copy, scale=rstd[:])
-                nc.gpsimd.tensor_tensor(out=t[:], in0=t[:], in1=beta_bc[:], op=ALU.add)
-            nc.sync.dma_start(out=of[rb * P:(rb + 1) * P, :], in_=t[:])
+            ln[rb] = (mv, sd, rstd, t)
 
-        xg0 = xgp.tile([P, 4, 512, 4], BF16, align_bytes=64, name="xg")
-        for rb in range(4):
-            x_block(rb, xg0)
-        x_quant(0, xg0)
-        w_prep(0)
-        w_prep(1)
-        xg1 = xgp.tile([P, 4, 512, 4], BF16, align_bytes=64, name="xg")
-        for oc in range(16):
-            if oc + 2 < 16:
-                w_prep(oc + 2)
-            if oc in (1, 4, 7, 10):
-                x_block(4 + (oc - 1) // 3, xg1)
-            if oc == 12:
-                x_quant(1, xg1)
-            mx_t1(oc, 0)
+        def ln_exit(rb):
+            mv, sd, rstd, t = ln[rb]
+            for j in range(4):
+                nc.vector.scalar_tensor_tensor(out=t[:, j * 512:(j + 1) * 512], in0=banks[rb, j][:], scalar=mv[:, 0:1],
+                                               in1=g_bc[:, j * 512:(j + 1) * 512], op0=ALU.subtract, op1=ALU.mult)
+            nc.vector.reciprocal(out=rstd[:], in_=sd[:])
+
+        def ln_scale(rb, j):
+            mv, sd, rstd, t = ln[rb]
+            cols = slice(j * 512, (j + 1) * 512)
+            nc.scalar.activation(out=t[:, cols], in_=t[:, cols], func=ACT.Copy, scale=rstd[:])
+
+        def ln_add_store(rb, c):
+            mv, sd, rstd, t = ln[rb]
+            cols = slice(c * 1024, (c + 1) * 1024)
+            if rb == 7:
+                nc.vector.scalar_tensor_tensor(out=t[:, cols], in0=t[:, cols], scalar=rstd[:], in1=beta_bc[:, cols], op0=ALU.mult, op1=ALU.add)
+            else:
+                nc.gpsimd.tensor_tensor(out=t[:, cols], in0=t[:, cols], in1=beta_bc[:, cols], op=ALU.add)
+            nc.sync.dma_start(out=of[rb * P:(rb + 1) * P, cols], in_=t[:, cols])
+
+        for kind, i in (("x", 0), ("w", 0), ("x", 1), ("w", 1), ("x", 2), ("w", 2), ("x", 3), ("w", 3), ("w", 4), ("w", 5)):
+            (load_x if kind == "x" else load_w)(i)
+        xgs = {}
+
+        def x_half(b):
+            if b % 2 == 0:
+                xgs[b // 2] = xgp.tile([P, 4, 256, 4], BF16, align_bytes=64, name="xg")
+            x_mult(b, xgs[b // 2])
+
+        pz = psa.tile([P, 512], F32, tag="a", name="pz")
+        nc.tensor.transpose(pz[:, 0:P], cz[:], ident_f[:])
+        nc.vector.tensor_copy(out=isc_w[:], in_=pz[:, 0:8])
+        transposes(xb[0], ("x", 0))
+        x_half(0)
+        transposes(wt[0], ("w", 0))
+        w_exit(0)
+        transposes(xb[1], ("x", 1))
+        x_half(1)
+        x_quant(0, xgs[0])
+        transposes(wt[1], ("w", 1))
+        w_exit(1)
+        w_quant(0)
+        transposes(xb[2], ("x", 2))
+        x_half(2)
+        pb = psa.tile([P, 1024], BF16, tag="a", name="pb")
+        nc.tensor.transpose(pb[:, 0:P], cb[:], ident_b[:])
+        nc.vector.tensor_copy(out=ob[:], in_=pb[:, 0:32])
+        transposes(wt[2], ("w", 2))
+        w_exit(2)
+        w_quant(1)
+        late = [("w", 6), ("w", 7), ("x", 4), ("w", 8), ("x", 5), ("w", 9), ("w", 10), ("x", 6), ("w", 11), ("x", 7), ("w", 12), ("w", 13), ("w", 14), ("w", 15)]
+        rest = [(o, q) for q in range(1, 4) for o in range(16)]
+        extra = EXTRA
+        for s in range(16):
+            for kind, i in late[2 * s:2 * s + 2]:
+                (load_x if kind == "x" else load_w)(i)
+            o = s + AHEAD
+            if o < 16:
+                transposes(wt[o], ("w", o))
+            mx(s, 0)
+            if s in X_AT:
+                transposes(xb[X_AT[s]], ("x", X_AT[s]))
+            if o < 16:
+                w_exit(o)
+            if o - 1 < 16:
+                w_quant(o - 1)
+            if s in X_AT:
+                x_half(X_AT[s])
+                if X_AT[s] % 2:
+                    x_quant(X_AT[s] // 2, xgs[X_AT[s] // 2])
+            affine(s, 0)
+            if s >= EXTRA_FROM:
+                for i in range(min(extra, -(-extra // (16 - s)))):
+                    unit = rest.pop(0)
+                    mx(*unit)
+                    affine(*unit)
+                    extra -= 1
         g_bc = win.tile([P, DO], BF16, tag="wt", name="g_bc")
         nc.sync.dma_start(out=g_bc[:], in_=ln_gamma.partition_broadcast(P))
         beta_bc = win.tile([P, DO], BF16, tag="wt", name="beta_bc")
         nc.sync.dma_start(out=beta_bc[:], in_=ln_beta.partition_broadcast(P))
-        for i in range(4):
-            for oc in range(4 * i, 4 * i + 4):
-                mx_t1(oc, 1)
-            ln_block(i, g_bc, beta_bc)
-        for i in range(4, 8):
-            ln_block(i, g_bc, beta_bc)
+        for j in range(4):
+            ln_tr(0, j)
+        for b in range(8):
+            todo = [rest.pop(0) for i in range(min(UNITS, len(rest)))]
+            open_units = []
+
+            def unit(n):
+                for i in range(min(n, len(todo))):
+                    u = todo.pop(0)
+                    mx(*u)
+                    open_units.append(u)
+
+            def close(n):
+                for i in range(min(n, len(open_units))):
+                    affine(*open_units.pop(0))
+
+            if b < 7:
+                ln_tr(b + 1, 0)
+            unit(2)
+            if b > 0:
+                ln_scale(b - 1, 0)
+            close(1)
+            if b > 0:
+                ln_scale(b - 1, 1)
+                ln_add_store(b - 1, 0)
+            close(1)
+            unit(1)
+            if b < 7:
+                ln_tr(b + 1, 1)
+            if b > 0:
+                ln_scale(b - 1, 2)
+            unit(1)
+            close(1)
+            if b > 0:
+                ln_scale(b - 1, 3)
+                ln_add_store(b - 1, 1)
+            close(1)
+            ln_stats(b)
+            ln_exit(b)
+            unit(1)
+            close(1)
+            if b < 7:
+                ln_tr(b + 1, 2)
+            unit(UNITS)
+            close(UNITS)
+            if b < 7:
+                ln_tr(b + 1, 3)
+        ln_add_store(7, 0)
+        ln_add_store(7, 1)

@@ -20,9 +20,8 @@ TINY = 2.0 ** -40
 W_ON_V = (3, 6, 9, 12, 14)
 AHEAD = 3
 X_AT = {1: 3, 4: 4, 7: 5, 10: 6, 13: 7}
-EXTRA_FROM = 5
-EXTRA = 6
-UNITS = 7
+EXTRA_AT = (3, 5, 7, 9, 11, 13)
+PAIRS = 3
 
 
 def tile_onebitlinear_kernel(tc, x, weight, in_channel_scale, out_channel_scale, bias, ln_gamma, ln_beta, out):
@@ -54,7 +53,7 @@ def tile_onebitlinear_kernel(tc, x, weight, in_channel_scale, out_channel_scale,
         nc.scalar.dma_start(out=cb[0:16, :], in_=out_channel_scale.rearrange("(a b) -> a b", a=16))
         nc.scalar.dma_start(out=cb[16:32, :], in_=bias.rearrange("(a b) -> a b", a=16))
         warm = const.tile([P, 1], F32, name="warm")
-        nc.scalar.activation(out=warm[:], in_=tiny[:], func=ACT.Sign)
+        nc.scalar.activation(out=warm[:], in_=eps[:], func=ACT.Abs_reciprocal_sqrt)
         ident_f = const.tile([P, P], F32, name="ident_f")
         make_identity(nc, ident_f[:])
         ident_b = const.tile([P, P], BF16, name="ident_b")
@@ -111,18 +110,19 @@ def tile_onebitlinear_kernel(tc, x, weight, in_channel_scale, out_channel_scale,
                     in_=xg[:, 2 * j:2 * j + 2, :, :].rearrange("p g r t -> p (g r t)"),
                 )
 
-        def w_exit(oc):
-            wg[oc] = wgp.tile([P, DI], BF16, align_bytes=64, name="wg")
-            for g in range(4):
-                tp = tps[("w", oc), g // 2]
-                gl = g % 2
+        def w_exit(oc, hb):
+            if hb == 0:
+                wg[oc] = wgp.tile([P, DI], BF16, align_bytes=64, name="wg")
+            tp = tps[("w", oc), hb]
+            for gl in range(2):
+                g = 2 * hb + gl
                 dst = wg[oc][:, g * 512:(g + 1) * 512].rearrange("p (o u e) -> p o u e", u=2, e=2)
                 src = tp[:, gl * 256:(gl + 1) * 256].bitcast(BF16).rearrange("p (u o e) -> p o u e", u=2, e=2)
                 if oc in W_ON_V:
                     nc.vector.tensor_scalar(out=dst, in0=src, scalar1=0.0, scalar2=2.0, op0=ALU.is_ge, op1=ALU.mult)
                 else:
                     nc.scalar.activation(out=dst, in_=src, func=ACT.Sign, scale=BIG, bias=tiny[:])
-            if oc in W_ON_V:
+            if oc in W_ON_V and hb == 1:
                 nc.vector.tensor_scalar_add(out=wg[oc][:], in0=wg[oc][:], scalar1=-1.0)
 
         def w_quant(oc):
@@ -132,20 +132,22 @@ def tile_onebitlinear_kernel(tc, x, weight, in_channel_scale, out_channel_scale,
                 in_=wg[oc][:],
             )
 
-        def mx(oc, q):
-            a = psm.tile([P, 256], F32, name="acc")
-            for g in range(4):
-                nc.tensor.matmul_mx(
-                    out=a[:],
-                    lhsT=wc[:, oc, g, :].bitcast(FP8X4), lhsT_scale=wsc[:, oc, g, :],
-                    rhs=xc[:, q, g, :].bitcast(FP8X4), rhs_scale=xsc[:, q, g, :],
-                    start=(g == 0), stop=(g == 3),
-                )
+        def mx(oc, q, n):
+            a = psm.tile([P, 512], F32, name="acc")
+            for i in range(n):
+                for g in range(4):
+                    nc.tensor.matmul_mx(
+                        out=a[:, i * 256:(i + 1) * 256],
+                        lhsT=wc[:, oc + i, g, :].bitcast(FP8X4), lhsT_scale=wsc[:, oc + i, g, :],
+                        rhs=xc[:, q, g, :].bitcast(FP8X4), rhs_scale=xsc[:, q, g, :],
+                        start=(g == 0), stop=(g == 3),
+                    )
             acc[oc, q] = a
 
-        def affine(oc, q):
-            nc.scalar.activation(out=hT[:, oc, q * 256:(q + 1) * 256], in_=acc[oc, q][:], func=ACT.Identity,
-                                 scale=ob[:, oc:oc + 1], bias=ob[:, 16 + oc:17 + oc])
+        def affine(oc, q, n):
+            for i in range(n):
+                nc.scalar.activation(out=hT[:, oc + i, q * 256:(q + 1) * 256], in_=acc[oc, q][:, i * 256:(i + 1) * 256], func=ACT.Identity,
+                                     scale=ob[:, oc + i:oc + i + 1], bias=ob[:, 16 + oc + i:17 + oc + i])
 
         def ln_tr(rb, j):
             bank = psa.tile([P, 512], F32, tag="a", name="hn")
@@ -159,32 +161,34 @@ def tile_onebitlinear_kernel(tc, x, weight, in_channel_scale, out_channel_scale,
                 nc.vector.bn_stats(out=st[:, j, :], in_=banks[rb, j][:])
             mv = small.tile([P, 2], F32, name="mv")
             nc.vector.bn_aggr(out=mv[:], in_=st[:].rearrange("p a b -> p (a b)"))
-            sd = small.tile([P, 1], F32, name="sd")
-            nc.scalar.activation(out=sd[:], in_=mv[:, 1:2], func=ACT.Sqrt, bias=eps[:], scale=1.0)
             rstd = small.tile([P, 1], F32, name="rstd")
+            nc.scalar.activation(out=rstd[:], in_=mv[:, 1:2], func=ACT.Abs_reciprocal_sqrt, bias=eps[:], scale=1.0)
             t = res.tile([P, DO], F32, name="t")
-            ln[rb] = (mv, sd, rstd, t)
+            ln[rb] = (mv, rstd, t)
 
         def ln_exit(rb):
-            mv, sd, rstd, t = ln[rb]
+            mv, rstd, t = ln[rb]
             for j in range(4):
                 nc.vector.scalar_tensor_tensor(out=t[:, j * 512:(j + 1) * 512], in0=banks[rb, j][:], scalar=mv[:, 0:1],
                                                in1=g_bc[:, j * 512:(j + 1) * 512], op0=ALU.subtract, op1=ALU.mult)
-            nc.vector.reciprocal(out=rstd[:], in_=sd[:])
 
         def ln_scale(rb, j):
-            mv, sd, rstd, t = ln[rb]
+            mv, rstd, t = ln[rb]
             cols = slice(j * 512, (j + 1) * 512)
             nc.scalar.activation(out=t[:, cols], in_=t[:, cols], func=ACT.Copy, scale=rstd[:])
 
         def ln_add_store(rb, c):
-            mv, sd, rstd, t = ln[rb]
+            mv, rstd, t = ln[rb]
             cols = slice(c * 1024, (c + 1) * 1024)
-            if rb == 7:
-                nc.vector.scalar_tensor_tensor(out=t[:, cols], in0=t[:, cols], scalar=rstd[:], in1=beta_bc[:, cols], op0=ALU.mult, op1=ALU.add)
-            else:
-                nc.gpsimd.tensor_tensor(out=t[:, cols], in0=t[:, cols], in1=beta_bc[:, cols], op=ALU.add)
+            nc.gpsimd.tensor_tensor(out=t[:, cols], in0=t[:, cols], in1=beta_bc[:, cols], op=ALU.add)
             nc.sync.dma_start(out=of[rb * P:(rb + 1) * P, cols], in_=t[:, cols])
+
+        def ln_last(rb):
+            mv, rstd, t = ln[rb]
+            for j in range(4):
+                cols = slice(j * 512, (j + 1) * 512)
+                nc.vector.scalar_tensor_tensor(out=t[:, cols], in0=t[:, cols], scalar=rstd[:], in1=beta_bc[:, cols], op0=ALU.mult, op1=ALU.add)
+                nc.sync.dma_start(out=of[rb * P:(rb + 1) * P, cols], in_=t[:, cols])
 
         for kind, i in (("x", 0), ("w", 0), ("x", 1), ("w", 1), ("x", 2), ("w", 2), ("x", 3), ("w", 3), ("w", 4), ("w", 5)):
             (load_x if kind == "x" else load_w)(i)
@@ -201,12 +205,14 @@ def tile_onebitlinear_kernel(tc, x, weight, in_channel_scale, out_channel_scale,
         transposes(xb[0], ("x", 0))
         x_half(0)
         transposes(wt[0], ("w", 0))
-        w_exit(0)
+        w_exit(0, 0)
+        w_exit(0, 1)
         transposes(xb[1], ("x", 1))
         x_half(1)
         x_quant(0, xgs[0])
         transposes(wt[1], ("w", 1))
-        w_exit(1)
+        w_exit(1, 0)
+        w_exit(1, 1)
         w_quant(0)
         transposes(xb[2], ("x", 2))
         x_half(2)
@@ -214,35 +220,45 @@ def tile_onebitlinear_kernel(tc, x, weight, in_channel_scale, out_channel_scale,
         nc.tensor.transpose(pb[:, 0:P], cb[:], ident_b[:])
         nc.vector.tensor_copy(out=ob[:], in_=pb[:, 0:32])
         transposes(wt[2], ("w", 2))
-        w_exit(2)
+        w_exit(2, 0)
+        w_exit(2, 1)
         w_quant(1)
         late = [("w", 6), ("w", 7), ("x", 4), ("w", 8), ("x", 5), ("w", 9), ("w", 10), ("x", 6), ("w", 11), ("x", 7), ("w", 12), ("w", 13), ("w", 14), ("w", 15)]
-        rest = [(o, q) for q in range(1, 4) for o in range(16)]
-        extra = EXTRA
+        rest = [(o, q, 2) for q in range(1, 4) for o in range(0, 16, 2)]
+        open_units = []
+
+        def close(n):
+            for i in range(min(n, len(open_units))):
+                affine(*open_units.pop(0))
+
         for s in range(16):
             for kind, i in late[2 * s:2 * s + 2]:
                 (load_x if kind == "x" else load_w)(i)
             o = s + AHEAD
+            before = len(open_units)
             if o < 16:
                 transposes(wt[o], ("w", o))
-            mx(s, 0)
+            mx(s, 0, 1)
+            open_units.append((s, 0, 1))
             if s in X_AT:
                 transposes(xb[X_AT[s]], ("x", X_AT[s]))
+            if s in EXTRA_AT:
+                u = rest.pop(0)
+                mx(*u)
+                open_units.append(u)
+            close(before)
             if o < 16:
-                w_exit(o)
+                w_exit(o, 0)
+            close(1)
+            if o < 16:
+                w_exit(o, 1)
             if o - 1 < 16:
                 w_quant(o - 1)
             if s in X_AT:
                 x_half(X_AT[s])
                 if X_AT[s] % 2:
                     x_quant(X_AT[s] // 2, xgs[X_AT[s] // 2])
-            affine(s, 0)
-            if s >= EXTRA_FROM:
-                for i in range(min(extra, -(-extra // (16 - s)))):
-                    unit = rest.pop(0)
-                    mx(*unit)
-                    affine(*unit)
-                    extra -= 1
+        close(len(open_units))
         g_bc = win.tile([P, DO], BF16, tag="wt", name="g_bc")
         nc.sync.dma_start(out=g_bc[:], in_=ln_gamma.partition_broadcast(P))
         beta_bc = win.tile([P, DO], BF16, tag="wt", name="beta_bc")
@@ -250,49 +266,33 @@ def tile_onebitlinear_kernel(tc, x, weight, in_channel_scale, out_channel_scale,
         for j in range(4):
             ln_tr(0, j)
         for b in range(8):
-            todo = [rest.pop(0) for i in range(min(UNITS, len(rest)))]
-            open_units = []
-
-            def unit(n):
-                for i in range(min(n, len(todo))):
-                    u = todo.pop(0)
-                    mx(*u)
-                    open_units.append(u)
-
-            def close(n):
-                for i in range(min(n, len(open_units))):
-                    affine(*open_units.pop(0))
-
+            todo = [rest.pop(0) for i in range(min(PAIRS, len(rest)))]
             if b < 7:
                 ln_tr(b + 1, 0)
-            unit(2)
+                ln_tr(b + 1, 1)
+            for u in todo[:2]:
+                mx(*u)
             if b > 0:
                 ln_scale(b - 1, 0)
-            close(1)
-            if b > 0:
                 ln_scale(b - 1, 1)
                 ln_add_store(b - 1, 0)
-            close(1)
-            unit(1)
-            if b < 7:
-                ln_tr(b + 1, 1)
+            for u in todo[:1]:
+                affine(*u)
             if b > 0:
                 ln_scale(b - 1, 2)
-            unit(1)
-            close(1)
-            if b > 0:
                 ln_scale(b - 1, 3)
                 ln_add_store(b - 1, 1)
-            close(1)
             ln_stats(b)
+            for u in todo[1:2]:
+                affine(*u)
             ln_exit(b)
-            unit(1)
-            close(1)
-            if b < 7:
+            if b < 7 and b % 2 == 0:
                 ln_tr(b + 1, 2)
-            unit(UNITS)
-            close(UNITS)
-            if b < 7:
                 ln_tr(b + 1, 3)
-        ln_add_store(7, 0)
-        ln_add_store(7, 1)
+            for u in todo[2:]:
+                mx(*u)
+                affine(*u)
+            if b < 7 and b % 2 == 1:
+                ln_tr(b + 1, 2)
+                ln_tr(b + 1, 3)
+        ln_last(7)

@@ -19,7 +19,8 @@ BIG = 2.0 ** 100
 TINY = 2.0 ** -40
 W_ON_V = (3, 6, 9, 12, 14)
 AHEAD = 3
-X_AT = {1: 3, 4: 4, 7: 5, 10: 6, 13: 7}
+X_AT = {1: 3, 4: 4, 7: 5, 10: 6, 12: 7}
+EARLY = {13: (0, 1), 15: (2,)}
 EXTRA_AT = (3, 5, 7, 9, 11, 13)
 PAIRS = 3
 
@@ -43,7 +44,6 @@ def tile_onebitlinear_kernel(tc, x, weight, in_channel_scale, out_channel_scale,
 
         cz = const.tile([P, P], F32, name="cz")
         nc.vector.memset(cz[:], 0.0)
-        nc.sync.dma_start(out=cz[0:8, :].bitcast(BF16), in_=in_channel_scale.rearrange("(a b) -> a b", a=8))
         tiny = const.tile([P, 1], F32, name="tiny")
         nc.vector.memset(tiny[:], TINY)
         eps = const.tile([P, 1], F32, name="eps")
@@ -72,7 +72,12 @@ def tile_onebitlinear_kernel(tc, x, weight, in_channel_scale, out_channel_scale,
 
         def load_x(rb):
             t = xin.tile([P, DI], BF16, name="xb")
-            nc.sync.dma_start(out=t[:], in_=xf[rb * P:(rb + 1) * P, :])
+            if rb == 0:
+                nc.sync.dma_start(out=t[:, 0:DI // 2], in_=xf[0:P, 0:DI // 2])
+                nc.sync.dma_start(out=cz[0:8, :].bitcast(BF16), in_=in_channel_scale.rearrange("(a b) -> a b", a=8))
+                nc.sync.dma_start(out=t[:, DI // 2:DI], in_=xf[0:P, DI // 2:DI])
+            else:
+                nc.sync.dma_start(out=t[:], in_=xf[rb * P:(rb + 1) * P, :])
             xb[rb] = t
 
         def load_w(oc):
@@ -155,10 +160,16 @@ def tile_onebitlinear_kernel(tc, x, weight, in_channel_scale, out_channel_scale,
                 nc.tensor.transpose(bank[:, q * P:(q + 1) * P], hT[:, 4 * j + q, rb * P:(rb + 1) * P], ident_f[:])
             banks[rb, j] = bank
 
+        def ln_bn(rb, j):
+            if j == 0:
+                stat[rb] = small.tile([P, 4, 6], F32, name="st")
+            nc.vector.bn_stats(out=stat[rb][:, j, :], in_=banks[rb, j][:])
+
         def ln_stats(rb):
-            st = small.tile([P, 4, 6], F32, name="st")
             for j in range(4):
-                nc.vector.bn_stats(out=st[:, j, :], in_=banks[rb, j][:])
+                if rb > 0 or j == 3:
+                    ln_bn(rb, j)
+            st = stat[rb]
             mv = small.tile([P, 2], F32, name="mv")
             nc.vector.bn_aggr(out=mv[:], in_=st[:].rearrange("p a b -> p (a b)"))
             rstd = small.tile([P, 1], F32, name="rstd")
@@ -199,10 +210,10 @@ def tile_onebitlinear_kernel(tc, x, weight, in_channel_scale, out_channel_scale,
                 xgs[b // 2] = xgp.tile([P, 4, 256, 4], BF16, align_bytes=64, name="xg")
             x_mult(b, xgs[b // 2])
 
+        transposes(xb[0], ("x", 0))
         pz = psa.tile([P, 512], F32, tag="a", name="pz")
         nc.tensor.transpose(pz[:, 0:P], cz[:], ident_f[:])
         nc.vector.tensor_copy(out=isc_w[:], in_=pz[:, 0:8])
-        transposes(xb[0], ("x", 0))
         x_half(0)
         transposes(wt[0], ("w", 0))
         w_exit(0, 0)
@@ -258,13 +269,15 @@ def tile_onebitlinear_kernel(tc, x, weight, in_channel_scale, out_channel_scale,
                 x_half(X_AT[s])
                 if X_AT[s] % 2:
                     x_quant(X_AT[s] // 2, xgs[X_AT[s] // 2])
+            for j in EARLY.get(s, ()):
+                ln_tr(0, j)
+                ln_bn(0, j)
         close(len(open_units))
         g_bc = win.tile([P, DO], BF16, tag="wt", name="g_bc")
         nc.sync.dma_start(out=g_bc[:], in_=ln_gamma.partition_broadcast(P))
         beta_bc = win.tile([P, DO], BF16, tag="wt", name="beta_bc")
         nc.sync.dma_start(out=beta_bc[:], in_=ln_beta.partition_broadcast(P))
-        for j in range(4):
-            ln_tr(0, j)
+        ln_tr(0, 3)
         for b in range(8):
             todo = [rest.pop(0) for i in range(min(PAIRS, len(rest)))]
             if b < 7:
@@ -273,19 +286,19 @@ def tile_onebitlinear_kernel(tc, x, weight, in_channel_scale, out_channel_scale,
             for u in todo[:2]:
                 mx(*u)
             if b > 0:
-                ln_scale(b - 1, 0)
-                ln_scale(b - 1, 1)
-                ln_add_store(b - 1, 0)
-            for u in todo[:1]:
-                affine(*u)
-            if b > 0:
                 ln_scale(b - 1, 2)
                 ln_scale(b - 1, 3)
                 ln_add_store(b - 1, 1)
+            for u in todo[:1]:
+                affine(*u)
             ln_stats(b)
             for u in todo[1:2]:
                 affine(*u)
             ln_exit(b)
+            if b < 7:
+                ln_scale(b, 0)
+                ln_scale(b, 1)
+                ln_add_store(b, 0)
             if b < 7 and b % 2 == 0:
                 ln_tr(b + 1, 2)
                 ln_tr(b + 1, 3)

from contextlib import ExitStack

import concourse.mybir as mybir
from concourse.masks import make_identity

F32 = mybir.dt.float32
BF16 = mybir.dt.bfloat16
U32 = mybir.dt.uint32
U8 = mybir.dt.uint8
FP8X4 = mybir.dt.float8_e4m3fn_x4
ALU = mybir.AluOpType
ACT = mybir.ActivationFunctionType

P = 128
R, DI, DO = 1024, 2048, 2048
FLOPS = 2 * R * DI * DO
LN_EPS = 1e-5
BIG = 2.0 ** 100
TINY = 2.0 ** -40
W_ON_V = (3, 6, 9, 12, 14)
AHEAD = 3
X_AT = {1: 3, 4: 4, 7: 5, 10: 6, 12: 7}
EARLY = {13: (0, 1), 15: (2,)}
EXTRA_AT = (3, 5, 7, 9, 11, 13)
PAIRS = 3


def tile_onebitlinear_kernel(tc, x, weight, in_channel_scale, out_channel_scale, bias, ln_gamma, ln_beta, out):
    nc = tc.nc
    xf = x.flatten_outer_dims()
    of = out.flatten_outer_dims()
    with ExitStack() as es:
        const = es.enter_context(tc.tile_pool(name="const", bufs=1))
        keep = es.enter_context(tc.tile_pool(name="keep", bufs=1))
        xin = es.enter_context(tc.tile_pool(name="xin", bufs=4))
        xgp = es.enter_context(tc.tile_pool(name="xgp", bufs=2))
        win = es.enter_context(tc.tile_pool(name="win", bufs=6))
        wgp = es.enter_context(tc.tile_pool(name="wgp", bufs=4))
        res = es.enter_context(tc.tile_pool(name="res", bufs=3))
        small = es.enter_context(tc.tile_pool(name="small", bufs=4))
        psa = es.enter_context(tc.psum_pool(name="psa", bufs=6))
        psm = es.enter_context(tc.psum_pool(name="psm", bufs=2))
        es.enter_context(tc.manual_schedule())

        cz = const.tile([P, P], F32, name="cz")
        nc.vector.memset(cz[:], 0.0)
        tiny = const.tile([P, 1], F32, name="tiny")
        nc.vector.memset(tiny[:], TINY)
        eps = const.tile([P, 1], F32, name="eps")
        nc.vector.memset(eps[:], LN_EPS)
        cb = const.tile([P, P], BF16, name="cb")
        nc.vector.memset(cb[:], 0.0)
        nc.scalar.dma_start(out=cb[0:16, :], in_=out_channel_scale.rearrange("(a b) -> a b", a=16))
        nc.scalar.dma_start(out=cb[16:32, :], in_=bias.rearrange("(a b) -> a b", a=16))
        warm = const.tile([P, 1], F32, name="warm")
        nc.scalar.activation(out=warm[:], in_=eps[:], func=ACT.Abs_reciprocal_sqrt)
        ident_f = const.tile([P, P], F32, name="ident_f")
        make_identity(nc, ident_f[:])
        ident_b = const.tile([P, P], BF16, name="ident_b")
        make_identity(nc, ident_b[:])
        isc_w = const.tile([P, 8], F32, name="isc_w")
        isc = isc_w[:].bitcast(BF16)
        ob = const.tile([P, 32], F32, name="ob")

        xc = keep.tile([P, 4, 4, 256], U32, align_bytes=64, name="xc")
        xsc = keep.tile([P, 4, 4, 256], U8, align_bytes=64, name="xsc")
        wc = keep.tile([P, 16, 4, P], U32, align_bytes=64, name="wc")
        wsc = keep.tile([P, 16, 4, P], U8, align_bytes=64, name="wsc")
        hT = keep.tile([P, 16, R], F32, name="hT")

        xb, wt, tps, wg, acc, banks, stat, ln = {}, {}, {}, {}, {}, {}, {}, {}

        def load_x(rb):
            t = xin.tile([P, DI], BF16, name="xb")
            if rb == 0:
                nc.sync.dma_start(out=t[:, 0:DI // 2], in_=xf[0:P, 0:DI // 2])
                nc.sync.dma_start(out=cz[0:8, :].bitcast(BF16), in_=in_channel_scale.rearrange("(a b) -> a b", a=8))
                nc.sync.dma_start(out=t[:, DI // 2:DI], in_=xf[0:P, DI // 2:DI])
            else:
                nc.sync.dma_start(out=t[:], in_=xf[rb * P:(rb + 1) * P, :])
            xb[rb] = t

        def load_w(oc):
            t = win.tile([P, DI], BF16, tag="wt", name="wt")
            nc.sync.dma_start(out=t[:], in_=weight[oc * P:(oc + 1) * P, :])
            wt[oc] = t

        def transposes(src, key):
            words = src[:].bitcast(F32)
            for hb in range(2):
                tp = psa.tile([P, 512], F32, tag="a", name="tp")
                for s in range(4):
                    a = 4 * hb + s
                    nc.tensor.transpose(tp[:, s * P:(s + 1) * P], words[:, a * P:(a + 1) * P], ident_f[:])
                tps[key, hb] = tp

        def x_mult(rb, xg):
            rl = rb % 2
            for hb in range(2):
                tp = tps[("x", rb), hb]
                for gl in range(2):
                    g = 2 * hb + gl
                    nc.vector.tensor_tensor(
                        out=xg[:, g, rl * P:(rl + 1) * P, :].rearrange("p r (u e) -> p r u e", u=2),
                        in0=tp[:, gl * 256:(gl + 1) * 256].bitcast(BF16).rearrange("p (u r e) -> p r u e", u=2, e=2),
                        in1=isc[:, 4 * g:4 * g + 4].rearrange("p (u e) -> p u e", u=2).unsqueeze(1).to_broadcast([P, P, 2, 2]),
                        op=ALU.mult,
                    )

        def x_quant(q, xg):
            for j in range(2):
                nc.vector.quantize_mx(
                    out=xc[:, q, 2 * j:2 * j + 2, :].rearrange("p g r -> p (g r)").bitcast(FP8X4),
                    scales=xsc[:, q, 2 * j:2 * j + 2, :].rearrange("p g r -> p (g r)"),
                    in_=xg[:, 2 * j:2 * j + 2, :, :].rearrange("p g r t -> p (g r t)"),
                )

        def w_exit(oc, hb):
            if hb == 0:
                wg[oc] = wgp.tile([P, DI], BF16, align_bytes=64, name="wg")
            tp = tps[("w", oc), hb]
            for gl in range(2):
                g = 2 * hb + gl
                dst = wg[oc][:, g * 512:(g + 1) * 512].rearrange("p (o u e) -> p o u e", u=2, e=2)
                src = tp[:, gl * 256:(gl + 1) * 256].bitcast(BF16).rearrange("p (u o e) -> p o u e", u=2, e=2)
                if oc in W_ON_V:
                    nc.vector.tensor_scalar(out=dst, in0=src, scalar1=0.0, scalar2=2.0, op0=ALU.is_ge, op1=ALU.mult)
                else:
                    nc.scalar.activation(out=dst, in_=src, func=ACT.Sign, scale=BIG, bias=tiny[:])
            if oc in W_ON_V and hb == 1:
                nc.vector.tensor_scalar_add(out=wg[oc][:], in0=wg[oc][:], scalar1=-1.0)

        def w_quant(oc):
            nc.vector.quantize_mx(
                out=wc[:, oc, :, :].rearrange("p g o -> p (g o)").bitcast(FP8X4),
                scales=wsc[:, oc, :, :].rearrange("p g o -> p (g o)"),
                in_=wg[oc][:],
            )

        def mx(oc, q, n):
            a = psm.tile([P, 512], F32, name="acc")
            for i in range(n):
                for g in range(4):
                    nc.tensor.matmul_mx(
                        out=a[:, i * 256:(i + 1) * 256],
                        lhsT=wc[:, oc + i, g, :].bitcast(FP8X4), lhsT_scale=wsc[:, oc + i, g, :],
                        rhs=xc[:, q, g, :].bitcast(FP8X4), rhs_scale=xsc[:, q, g, :],
                        start=(g == 0), stop=(g == 3),
                    )
            acc[oc, q] = a

        def affine(oc, q, n):
            for i in range(n):
                nc.scalar.activation(out=hT[:, oc + i, q * 256:(q + 1) * 256], in_=acc[oc, q][:, i * 256:(i + 1) * 256], func=ACT.Identity,
                                     scale=ob[:, oc + i:oc + i + 1], bias=ob[:, 16 + oc + i:17 + oc + i])

        def ln_tr(rb, j):
            bank = psa.tile([P, 512], F32, tag="a", name="hn")
            for q in range(4):
                nc.tensor.transpose(bank[:, q * P:(q + 1) * P], hT[:, 4 * j + q, rb * P:(rb + 1) * P], ident_f[:])
            banks[rb, j] = bank

        def ln_bn(rb, j):
            if j == 0:
                stat[rb] = small.tile([P, 4, 6], F32, name="st")
            nc.vector.bn_stats(out=stat[rb][:, j, :], in_=banks[rb, j][:])

        def ln_stats(rb):
            for j in range(4):
                if rb > 0 or j == 3:
                    ln_bn(rb, j)
            st = stat[rb]
            mv = small.tile([P, 2], F32, name="mv")
            nc.vector.bn_aggr(out=mv[:], in_=st[:].rearrange("p a b -> p (a b)"))
            rstd = small.tile([P, 1], F32, name="rstd")
            nc.scalar.activation(out=rstd[:], in_=mv[:, 1:2], func=ACT.Abs_reciprocal_sqrt, bias=eps[:], scale=1.0)
            t = res.tile([P, DO], F32, name="t")
            ln[rb] = (mv, rstd, t)

        def ln_exit(rb):
            mv, rstd, t = ln[rb]
            for j in range(4):
                nc.vector.scalar_tensor_tensor(out=t[:, j * 512:(j + 1) * 512], in0=banks[rb, j][:], scalar=mv[:, 0:1],
                                               in1=g_bc[:, j * 512:(j + 1) * 512], op0=ALU.subtract, op1=ALU.mult)

        def ln_scale(rb, j):
            mv, rstd, t = ln[rb]
            cols = slice(j * 512, (j + 1) * 512)
            nc.scalar.activation(out=t[:, cols], in_=t[:, cols], func=ACT.Copy, scale=rstd[:])

        def ln_add_store(rb, c):
            mv, rstd, t = ln[rb]
            cols = slice(c * 1024, (c + 1) * 1024)
            nc.gpsimd.tensor_tensor(out=t[:, cols], in0=t[:, cols], in1=beta_bc[:, cols], op=ALU.add)
            nc.sync.dma_start(out=of[rb * P:(rb + 1) * P, cols], in_=t[:, cols])

        def ln_last(rb):
            mv, rstd, t = ln[rb]
            for j in range(4):
                cols = slice(j * 512, (j + 1) * 512)
                nc.vector.scalar_tensor_tensor(out=t[:, cols], in0=t[:, cols], scalar=rstd[:], in1=beta_bc[:, cols], op0=ALU.mult, op1=ALU.add)
                nc.sync.dma_start(out=of[rb * P:(rb + 1) * P, cols], in_=t[:, cols])

        for kind, i in (("x", 0), ("w", 0), ("x", 1), ("w", 1), ("x", 2), ("w", 2), ("x", 3), ("w", 3), ("w", 4), ("w", 5)):
            (load_x if kind == "x" else load_w)(i)
        xgs = {}

        def x_half(b):
            if b % 2 == 0:
                xgs[b // 2] = xgp.tile([P, 4, 256, 4], BF16, align_bytes=64, name="xg")
            x_mult(b, xgs[b // 2])

        transposes(xb[0], ("x", 0))
        pz = psa.tile([P, 512], F32, tag="a", name="pz")
        nc.tensor.transpose(pz[:, 0:P], cz[:], ident_f[:])
        nc.vector.tensor_copy(out=isc_w[:], in_=pz[:, 0:8])
        x_half(0)
        transposes(wt[0], ("w", 0))
        w_exit(0, 0)
        w_exit(0, 1)
        transposes(xb[1], ("x", 1))
        x_half(1)
        x_quant(0, xgs[0])
        transposes(wt[1], ("w", 1))
        w_exit(1, 0)
        w_exit(1, 1)
        w_quant(0)
        transposes(xb[2], ("x", 2))
        x_half(2)
        pb = psa.tile([P, 1024], BF16, tag="a", name="pb")
        nc.tensor.transpose(pb[:, 0:P], cb[:], ident_b[:])
        nc.vector.tensor_copy(out=ob[:], in_=pb[:, 0:32])
        transposes(wt[2], ("w", 2))
        w_exit(2, 0)
        w_exit(2, 1)
        w_quant(1)
        late = [("w", 6), ("w", 7), ("x", 4), ("w", 8), ("x", 5), ("w", 9), ("w", 10), ("x", 6), ("w", 11), ("x", 7), ("w", 12), ("w", 13), ("w", 14), ("w", 15)]
        rest = [(o, q, 2) for q in range(1, 4) for o in range(0, 16, 2)]
        open_units = []

        def close(n):
            for i in range(min(n, len(open_units))):
                affine(*open_units.pop(0))

        for s in range(16):
            for kind, i in late[2 * s:2 * s + 2]:
                (load_x if kind == "x" else load_w)(i)
            o = s + AHEAD
            before = len(open_units)
            if o < 16:
                transposes(wt[o], ("w", o))
            mx(s, 0, 1)
            open_units.append((s, 0, 1))
            if s in X_AT:
                transposes(xb[X_AT[s]], ("x", X_AT[s]))
            if s in EXTRA_AT:
                u = rest.pop(0)
                mx(*u)
                open_units.append(u)
            close(before)
            if o < 16:
                w_exit(o, 0)
            close(1)
            if o < 16:
                w_exit(o, 1)
            if o - 1 < 16:
                w_quant(o - 1)
            if s in X_AT:
                x_half(X_AT[s])
                if X_AT[s] % 2:
                    x_quant(X_AT[s] // 2, xgs[X_AT[s] // 2])
            for j in EARLY.get(s, ()):
                ln_tr(0, j)
                ln_bn(0, j)
        close(len(open_units))
        g_bc = win.tile([P, DO], BF16, tag="wt", name="g_bc")
        nc.sync.dma_start(out=g_bc[:], in_=ln_gamma.partition_broadcast(P))
        beta_bc = win.tile([P, DO], BF16, tag="wt", name="beta_bc")
        nc.sync.dma_start(out=beta_bc[:], in_=ln_beta.partition_broadcast(P))
        ln_tr(0, 3)
        for b in range(8):
            todo = [rest.pop(0) for i in range(min(PAIRS, len(rest)))]
            if b < 7:
                ln_tr(b + 1, 0)
                ln_tr(b + 1, 1)
            for u in todo[:2]:
                mx(*u)
            if b > 0:
                ln_scale(b - 1, 2)
                ln_scale(b - 1, 3)
                ln_add_store(b - 1, 1)
            for u in todo[:1]:
                affine(*u)
            ln_stats(b)
            for u in todo[1:2]:
                affine(*u)
            ln_exit(b)
            if b < 7:
                ln_scale(b, 0)
                ln_scale(b, 1)
                ln_add_store(b, 0)
            if b < 7 and b % 2 == 0:
                ln_tr(b + 1, 2)
                ln_tr(b + 1, 3)
            for u in todo[2:]:
                mx(*u)
                affine(*u)
            if b < 7 and b % 2 == 1:
                ln_tr(b + 1, 2)
                ln_tr(b + 1, 3)
        ln_last(7)
